import numpy as np
import ml_dtypes


def mxq(x, axis, fmt="e4m3"):
    dtype, down = {"e4m3": (ml_dtypes.float8_e4m3fn, 7), "e5m2": (ml_dtypes.float8_e5m2, 14)}[fmt]
    v = np.moveaxis(np.asarray(x, np.float32).astype(ml_dtypes.bfloat16).astype(np.float64), axis, -1)
    blocks = v.reshape(v.shape[:-1] + (-1, 32))
    amax = np.abs(blocks).max(-1, keepdims=True)
    byte = np.maximum(np.where(amax > 0, np.frexp(amax)[1] - 1 + 127, 0) - down, 1)
    scale = np.exp2(byte - 127.0)
    codes = (blocks / scale).astype(np.float32).astype(dtype).astype(np.float64)
    return np.moveaxis((codes * scale).reshape(v.shape), -1, axis)


WIDE = False


def mx_kscale(k):
    if not WIDE:
        return np.ones(k)
    levels = np.array([10, -10, 5, -5, 0])
    if k % 512:
        return np.exp2(np.random.permutation(np.resize(levels, k // 32))).repeat(32)
    a = np.empty((k // 512, 16))
    for p in range(k // 512):
        a[p, :8] = np.random.permutation(np.resize(levels, 8))
        for g in range(8):
            far = levels[np.abs(levels - a[p, g]) >= 10]
            a[p, g + 8] = far[np.random.randint(len(far))]
    return np.exp2(a.ravel()).repeat(32)


BF16 = ml_dtypes.bfloat16


def bf(x):
    return np.asarray(x, np.float32).astype(BF16)


def f64(x):
    return np.asarray(x).astype(np.float64)


B, S, C, H, D = 8, 1024, 512, 2, 128
E = H * D


def rope_tables():
    inv_freq = 1.0 / (10000.0 ** (np.arange(0, D, 2) / D))
    emb = np.repeat(np.outer(np.arange(S), inv_freq), 2, axis=1)
    return np.cos(emb), np.sin(emb)


def rope(t, cos, sin):
    tr = t[..., 0::2]
    ti = t[..., 1::2]
    t_rot = np.stack([-ti, tr], axis=-1).reshape(t.shape)
    return t * cos + t_rot * sin


def setup_inputs():
    s = mx_kscale(C)
    cos, sin = rope_tables()
    return {"x": bf(np.random.standard_normal((B, S, C)) * s),
            "cos": bf(cos), "sin": bf(sin),
            "Wq": bf(np.random.standard_normal((E, C)) / np.sqrt(C) / s[None, :]),
            "bq": bf(np.random.standard_normal(E) * 0.1)}


def reference(x, cos, sin, Wq, bq):
    y = (mxq(f64(x), 2, "e4m3") @ mxq(f64(Wq), 1, "e4m3").T) + f64(bq)
    q = y.reshape(B, S, H, D).transpose(0, 2, 1, 3)
    return np.maximum(rope(q, f64(cos), f64(sin)), 0.0)

@@ -1,0 +1,189 @@
+from contextlib import ExitStack
+
+import concourse.mybir as mybir
+from concourse.masks import make_identity
+
+F32 = mybir.dt.float32
+BF16 = mybir.dt.bfloat16
+U32 = mybir.dt.uint32
+U8 = mybir.dt.uint8
+FP8X4 = mybir.dt.float8_e4m3fn_x4
+ALU = mybir.AluOpType
+ACT = mybir.ActivationFunctionType
+
+B, S, C, H, D = 8, 1024, 512, 2, 128
+P = 128
+PACK = 4
+WORDS = C // 2
+ROWS = S // P
+GROUP_ROWS = 4
+GROUP_TOKENS = GROUP_ROWS * P
+GROUPS = B * ROWS // GROUP_ROWS
+
+FLOPS = 2 * B * S * C * H * D
+
+
+def tile_lineartransformerblock_pa_t_kernel(tc, x, cos, sin, Wq, bq, out):
+    nc = tc.nc
+    with ExitStack() as ctx:
+        const = ctx.enter_context(tc.tile_pool(name="const", bufs=1))
+        tokens = ctx.enter_context(tc.tile_pool(name="tokens", bufs=GROUPS))
+        staged = ctx.enter_context(tc.tile_pool(name="staged", bufs=3))
+        products = ctx.enter_context(tc.tile_pool(name="products", bufs=3))
+        results = ctx.enter_context(tc.tile_pool(name="results", bufs=4))
+        psum_words = ctx.enter_context(tc.psum_pool(name="psum_words", bufs=2))
+        psum_proj = ctx.enter_context(tc.psum_pool(name="psum_proj", bufs=4))
+        psum_rope = ctx.enter_context(tc.psum_pool(name="psum_rope", bufs=2))
+        ctx.enter_context(tc.manual_schedule())
+
+        ident_f32 = const.tile([P, P], F32)
+        make_identity(nc, ident_f32[:])
+        ident_bf16 = const.tile([P, P], BF16)
+        make_identity(nc, ident_bf16[:])
+        swap_f32 = const.tile([P, P], F32)
+        ident_pairs = ident_f32[:].rearrange("k (i two) -> k i two", two=2)
+        swap_pairs = swap_f32[:].rearrange("k (i two) -> k i two", two=2)
+        nc.vector.tensor_copy(out=swap_pairs[:, :, 0], in_=ident_pairs[:, :, 1])
+        nc.vector.tensor_copy(out=swap_pairs[:, :, 1], in_=ident_pairs[:, :, 0])
+        bias_rows = const.tile([P, P], BF16)
+        nc.vector.memset(bias_rows[:], 0.0)
+
+        w_sb = const.tile([P, H, C], BF16)
+        nc.sync.dma_start(out=w_sb[:], in_=Wq.rearrange("(h d) k -> d h k", h=H))
+        nc.sync.dma_start(out=bias_rows[0:H, :], in_=bq.rearrange("(h d) -> h d", h=H))
+
+        x_tiles = {}
+
+        def load_tokens(g):
+            rows = slice((g % 2) * GROUP_ROWS, (g % 2 + 1) * GROUP_ROWS)
+            x_sb = tokens.tile([P, GROUP_ROWS, C], BF16)
+            nc.sync.dma_start(out=x_sb[:], in_=x[g // 2].rearrange("(p j) k -> p j k", j=ROWS)[:, rows, :])
+            x_tiles[g] = x_sb
+
+        load_tokens(0)
+        sin_sb = const.tile([P, ROWS, D], BF16)
+        nc.sync.dma_start(out=sin_sb[:], in_=sin.rearrange("(p j) d -> p j d", j=ROWS))
+        cos_sb = const.tile([P, ROWS, D], BF16)
+        nc.sync.dma_start(out=cos_sb[:], in_=cos.rearrange("(p j) d -> p j d", j=ROWS))
+        for g in range(1, GROUPS):
+            load_tokens(g)
+
+        def words_to_partitions(row_blocks, grouped_words):
+            words_ps = psum_words.tile([P, 2, 2 * P], F32, tag="words")
+            for r, block in enumerate(row_blocks):
+                for u in range(2):
+                    nc.tensor.transpose(words_ps[:, u, r * P : (r + 1) * P], block[:, u::2], ident_f32[:])
+            nc.scalar.copy(out=grouped_words, in_=words_ps[:].rearrange("p u c -> p c u"))
+
+        w_grouped = const.tile([P, H * D * PACK], BF16, align_bytes=64)
+        words_to_partitions(
+            [w_sb[:, h, :].bitcast(F32) for h in range(H)],
+            w_grouped[:].bitcast(F32).rearrange("p (c u) -> p c u", u=2),
+        )
+        w_codes = const.tile([P, H * D], U32, align_bytes=64)
+        w_scales = const.tile([P, H * D], U8, align_bytes=64)
+        nc.vector.quantize_mx(out=w_codes[:].bitcast(FP8X4), scales=w_scales[:], in_=w_grouped[:])
+
+        bias_ps = psum_rope.tile([P, P], BF16, tag="rope")
+        nc.tensor.transpose(bias_ps[:], bias_rows[:], ident_bf16[:])
+        bias = const.tile([P, H], F32)
+        nc.vector.tensor_copy(out=bias[:], in_=bias_ps[:, 0:H])
+
+        grouped_tiles = {}
+        code_tiles = {}
+        proj_tiles = {}
+        product_tiles = {}
+
+        def turn_tokens(g):
+            grouped = staged.tile([P, GROUP_TOKENS * PACK], BF16, align_bytes=64)
+            grouped_words = grouped[:].bitcast(F32).rearrange("p (c u) -> p c u", u=2)
+            for half in range(2):
+                words_to_partitions(
+                    [x_tiles[g][:, 2 * half + r, :].bitcast(F32) for r in range(2)],
+                    grouped_words[:, half * 2 * P : (half + 1) * 2 * P, :],
+                )
+            grouped_tiles[g] = grouped
+
+        def quantise(g):
+            codes = staged.tile([P, GROUP_TOKENS], U32, align_bytes=64)
+            scales = staged.tile([P, GROUP_TOKENS], U8, align_bytes=64)
+            nc.vector.quantize_mx(out=codes[:].bitcast(FP8X4), scales=scales[:], in_=grouped_tiles[g][:])
+            code_tiles[g] = (codes, scales)
+
+        def project(g):
+            codes, scales = code_tiles[g]
+            for h in range(H):
+                head = slice(h * D, (h + 1) * D)
+                y_ps = psum_proj.tile([P, GROUP_TOKENS], F32, tag="proj")
+                nc.tensor.matmul_mx(
+                    out=y_ps[:],
+                    lhsT=w_codes[:, head].bitcast(FP8X4),
+                    lhsT_scale=w_scales[:, head],
+                    rhs=codes[:].bitcast(FP8X4),
+                    rhs_scale=scales[:],
+                    start=True,
+                    stop=True,
+                )
+                proj_tiles[(g, h)] = y_ps
+
+        def rope_products(g, h):
+            cols = slice((g % 2) * GROUP_TOKENS, (g % 2 + 1) * GROUP_TOKENS)
+            y_ps = proj_tiles[(g, h)]
+            own = products.tile([P, GROUP_TOKENS], F32)
+            nc.vector.scalar_tensor_tensor(
+                out=own[:], in0=y_ps[:], scalar=bias[:, h : h + 1], in1=cos_t[:, cols], op0=ALU.add, op1=ALU.mult
+            )
+            lent = products.tile([P, GROUP_TOKENS], F32)
+            nc.vector.scalar_tensor_tensor(
+                out=lent[:], in0=y_ps[:], scalar=bias[:, h : h + 1], in1=sin_lent_t[:, cols], op0=ALU.add, op1=ALU.mult
+            )
+            product_tiles[(g, h)] = (own, lent)
+
+        def finish(g, h):
+            own, lent = product_tiles[(g, h)]
+            rope_ps = psum_rope.tile([P, GROUP_ROWS, D], F32, tag="rope")
+            for j in range(GROUP_ROWS):
+                block = slice(j * P, (j + 1) * P)
+                nc.tensor.matmul(rope_ps[:, j, :], lhsT=own[:, block], rhs=ident_f32[:], is_transpose=True, start=True, stop=False)
+                nc.tensor.matmul(rope_ps[:, j, :], lhsT=lent[:, block], rhs=swap_f32[:], is_transpose=True, start=False, stop=True)
+            out_sb = results.tile([P, GROUP_ROWS, D], F32)
+            nc.scalar.activation(out=out_sb[:], in_=rope_ps[:], func=ACT.Relu)
+            rows = slice((g % 2) * GROUP_ROWS, (g % 2 + 1) * GROUP_ROWS)
+            nc.sync.dma_start(out=out[g // 2, h].rearrange("(p j) d -> p j d", j=ROWS)[:, rows, :], in_=out_sb[:])
+
+        def table_to_channels(table_sb, table_t):
+            table_ps = psum_proj.tile([P, ROWS, P], BF16, tag="proj")
+            for j in range(ROWS):
+                nc.tensor.transpose(table_ps[:, j, :], table_sb[:, j, :], ident_bf16[:])
+            nc.scalar.copy(out=table_t[:], in_=table_ps[:].rearrange("d j p -> d (j p)"))
+
+        turn_tokens(0)
+        cos_t = const.tile([P, S], BF16)
+        table_to_channels(cos_sb, cos_t)
+        turn_tokens(1)
+        quantise(0)
+        project(0)
+        sin_lent = const.tile([P, ROWS, D], BF16)
+        sin_pairs = sin_sb[:].rearrange("p j (i two) -> p j i two", two=2)
+        lent_pairs = sin_lent[:].rearrange("p j (i two) -> p j i two", two=2)
+        nc.gpsimd.tensor_scalar(out=lent_pairs[:, :, :, 0], in0=sin_pairs[:, :, :, 1], scalar1=1.0, scalar2=0.0, op0=ALU.mult, op1=ALU.add)
+        nc.gpsimd.tensor_scalar(out=lent_pairs[:, :, :, 1], in0=sin_pairs[:, :, :, 0], scalar1=-1.0, scalar2=0.0, op0=ALU.mult, op1=ALU.add)
+        sin_lent_t = const.tile([P, S], BF16)
+        table_to_channels(sin_lent, sin_lent_t)
+        turn_tokens(2)
+        quantise(1)
+        project(1)
+
+        for g in range(GROUPS):
+            rope_products(g, 0)
+            if g >= 1:
+                finish(g - 1, 1)
+            if g + 3 < GROUPS:
+                turn_tokens(g + 3)
+            if g + 2 < GROUPS:
+                quantise(g + 2)
+            finish(g, 0)
+            if g + 2 < GROUPS:
+                project(g + 2)
+            rope_products(g, 1)
+        finish(GROUPS - 1, 1)

@@ -93,16 +93,21 @@ def tile_lineartransformerblock_pa_t_kernel(tc, x, cos, sin, Wq, bq, out):
         code_tiles = {}
         proj_tiles = {}
         product_tiles = {}
+        rope_tiles = {}
+
+        def turn_half(g, half):
+            if half == 0:
+                grouped_tile = staged.tile([P, GROUP_TOKENS * PACK], BF16, align_bytes=64)
+                grouped_tiles[g] = grouped_tile
+            grouped_words = grouped_tiles[g][:].bitcast(F32).rearrange("p (c u) -> p c u", u=2)
+            words_to_partitions(
+                [x_tiles[g][:, 2 * half + r, :].bitcast(F32) for r in range(2)],
+                grouped_words[:, half * 2 * P : (half + 1) * 2 * P, :],
+            )
 
         def turn_tokens(g):
-            grouped = staged.tile([P, GROUP_TOKENS * PACK], BF16, align_bytes=64)
-            grouped_words = grouped[:].bitcast(F32).rearrange("p (c u) -> p c u", u=2)
             for half in range(2):
-                words_to_partitions(
-                    [x_tiles[g][:, 2 * half + r, :].bitcast(F32) for r in range(2)],
-                    grouped_words[:, half * 2 * P : (half + 1) * 2 * P, :],
-                )
-            grouped_tiles[g] = grouped
+                turn_half(g, half)
 
         def quantise(g):
             codes = staged.tile([P, GROUP_TOKENS], U32, align_bytes=64)
@@ -139,13 +144,20 @@ def tile_lineartransformerblock_pa_t_kernel(tc, x, cos, sin, Wq, bq, out):
             )
             product_tiles[(g, h)] = (own, lent)
 
-        def finish(g, h):
+        def turn_back(g, h, rows, by_product=False):
+            if rows[0] == 0:
+                rope_tile = psum_rope.tile([P, GROUP_ROWS, D], F32, tag="rope")
+                rope_tiles[(g, h)] = rope_tile
+            rope_ps = rope_tiles[(g, h)]
             own, lent = product_tiles[(g, h)]
-            rope_ps = psum_rope.tile([P, GROUP_ROWS, D], F32, tag="rope")
-            for j in range(GROUP_ROWS):
+            turn = not by_product
+            for j in rows:
                 block = slice(j * P, (j + 1) * P)
-                nc.tensor.matmul(rope_ps[:, j, :], lhsT=own[:, block], rhs=ident_f32[:], is_transpose=True, start=True, stop=False)
-                nc.tensor.matmul(rope_ps[:, j, :], lhsT=lent[:, block], rhs=swap_f32[:], is_transpose=True, start=False, stop=True)
+                nc.tensor.matmul(rope_ps[:, j, :], lhsT=own[:, block], rhs=ident_f32[:], is_transpose=turn, start=True, stop=False)
+                nc.tensor.matmul(rope_ps[:, j, :], lhsT=lent[:, block], rhs=swap_f32[:], is_transpose=turn, start=False, stop=True)
+
+        def emit(g, h):
+            rope_ps = rope_tiles[(g, h)]
             out_sb = results.tile([P, GROUP_ROWS, D], F32)
             nc.scalar.activation(out=out_sb[:], in_=rope_ps[:], func=ACT.Relu)
             rows = slice((g % 2) * GROUP_ROWS, (g % 2 + 1) * GROUP_ROWS)
@@ -177,13 +189,20 @@ def tile_lineartransformerblock_pa_t_kernel(tc, x, cos, sin, Wq, bq, out):
         for g in range(GROUPS):
             rope_products(g, 0)
             if g >= 1:
-                finish(g - 1, 1)
+                turn_back(g - 1, 1, [0, 1, 2])
             if g + 3 < GROUPS:
-                turn_tokens(g + 3)
+                turn_half(g + 3, 0)
+            if g >= 1:
+                turn_back(g - 1, 1, [3], by_product=True)
+                emit(g - 1, 1)
+            if g + 3 < GROUPS:
+                turn_half(g + 3, 1)
             if g + 2 < GROUPS:
                 quantise(g + 2)
-            finish(g, 0)
+            turn_back(g, 0, [0, 1, 2, 3])
+            emit(g, 0)
             if g + 2 < GROUPS:
                 project(g + 2)
             rope_products(g, 1)
-        finish(GROUPS - 1, 1)
+        turn_back(GROUPS - 1, 1, [0, 1, 2, 3])
+        emit(GROUPS - 1, 1)

@@ -14,7 +14,7 @@ ACT = mybir.ActivationFunctionType
 B, S, C, H, D = 8, 1024, 512, 2, 128
 P = 128
 PACK = 4
-WORDS = C // 2
+PAIRS = D // 2
 ROWS = S // P
 GROUP_ROWS = 4
 GROUP_TOKENS = GROUP_ROWS * P
@@ -38,19 +38,11 @@ def tile_lineartransformerblock_pa_t_kernel(tc, x, cos, sin, Wq, bq, out):
 
         ident_f32 = const.tile([P, P], F32)
         make_identity(nc, ident_f32[:])
-        ident_bf16 = const.tile([P, P], BF16)
-        make_identity(nc, ident_bf16[:])
-        swap_f32 = const.tile([P, P], F32)
-        ident_pairs = ident_f32[:].rearrange("k (i two) -> k i two", two=2)
-        swap_pairs = swap_f32[:].rearrange("k (i two) -> k i two", two=2)
-        nc.vector.tensor_copy(out=swap_pairs[:, :, 0], in_=ident_pairs[:, :, 1])
-        nc.vector.tensor_copy(out=swap_pairs[:, :, 1], in_=ident_pairs[:, :, 0])
-        bias_rows = const.tile([P, P], BF16)
-        nc.vector.memset(bias_rows[:], 0.0)
+        bias_row = const.tile([P, H * D], BF16)
+        nc.vector.memset(bias_row[:], 0.0)
 
-        w_sb = const.tile([P, H, C], BF16)
-        nc.sync.dma_start(out=w_sb[:], in_=Wq.rearrange("(h d) k -> d h k", h=H))
-        nc.sync.dma_start(out=bias_rows[0:H, :], in_=bq.rearrange("(h d) -> h d", h=H))
+        w_sb = const.tile([P, 2, C], BF16)
+        nc.sync.dma_start(out=w_sb[:], in_=Wq.rearrange("(q e) k -> q e k", e=2))
 
         x_tiles = {}
 
@@ -61,10 +53,11 @@ def tile_lineartransformerblock_pa_t_kernel(tc, x, cos, sin, Wq, bq, out):
             x_tiles[g] = x_sb
 
         load_tokens(0)
-        sin_sb = const.tile([P, ROWS, D], BF16)
-        nc.sync.dma_start(out=sin_sb[:], in_=sin.rearrange("(p j) d -> p j d", j=ROWS))
+        nc.sync.dma_start(out=bias_row[0:1, :], in_=bq.rearrange("(o c) -> o c", o=1))
         cos_sb = const.tile([P, ROWS, D], BF16)
         nc.sync.dma_start(out=cos_sb[:], in_=cos.rearrange("(p j) d -> p j d", j=ROWS))
+        sin_sb = const.tile([P, ROWS, D], BF16)
+        nc.sync.dma_start(out=sin_sb[:], in_=sin.rearrange("(p j) d -> p j d", j=ROWS))
         for g in range(1, GROUPS):
             load_tokens(g)
 
@@ -75,25 +68,21 @@ def tile_lineartransformerblock_pa_t_kernel(tc, x, cos, sin, Wq, bq, out):
                     nc.tensor.transpose(words_ps[:, u, r * P : (r + 1) * P], block[:, u::2], ident_f32[:])
             nc.scalar.copy(out=grouped_words, in_=words_ps[:].rearrange("p u c -> p c u"))
 
-        w_grouped = const.tile([P, H * D * PACK], BF16, align_bytes=64)
+        w_grouped = const.tile([P, 2 * P * PACK], BF16, align_bytes=64)
         words_to_partitions(
-            [w_sb[:, h, :].bitcast(F32) for h in range(H)],
+            [w_sb[:, e, :].bitcast(F32) for e in range(2)],
             w_grouped[:].bitcast(F32).rearrange("p (c u) -> p c u", u=2),
         )
-        w_codes = const.tile([P, H * D], U32, align_bytes=64)
-        w_scales = const.tile([P, H * D], U8, align_bytes=64)
+        w_codes = const.tile([P, 2 * P], U32, align_bytes=64)
+        w_scales = const.tile([P, 2 * P], U8, align_bytes=64)
         nc.vector.quantize_mx(out=w_codes[:].bitcast(FP8X4), scales=w_scales[:], in_=w_grouped[:])
-
-        bias_ps = psum_rope.tile([P, P], BF16, tag="rope")
-        nc.tensor.transpose(bias_ps[:], bias_rows[:], ident_bf16[:])
-        bias = const.tile([P, H], F32)
-        nc.vector.tensor_copy(out=bias[:], in_=bias_ps[:, 0:H])
 
         grouped_tiles = {}
         code_tiles = {}
         proj_tiles = {}
         product_tiles = {}
         rope_tiles = {}
+        result_tiles = {}
 
         def turn_half(g, half):
             if half == 0:
@@ -105,10 +94,6 @@ def tile_lineartransformerblock_pa_t_kernel(tc, x, cos, sin, Wq, bq, out):
                 grouped_words[:, half * 2 * P : (half + 1) * 2 * P, :],
             )
 
-        def turn_tokens(g):
-            for half in range(2):
-                turn_half(g, half)
-
         def quantise(g):
             codes = staged.tile([P, GROUP_TOKENS], U32, align_bytes=64)
             scales = staged.tile([P, GROUP_TOKENS], U8, align_bytes=64)
@@ -117,92 +102,136 @@ def tile_lineartransformerblock_pa_t_kernel(tc, x, cos, sin, Wq, bq, out):
 
         def project(g):
             codes, scales = code_tiles[g]
-            for h in range(H):
-                head = slice(h * D, (h + 1) * D)
+            for e in range(2):
+                tile_cols = slice(e * P, (e + 1) * P)
                 y_ps = psum_proj.tile([P, GROUP_TOKENS], F32, tag="proj")
                 nc.tensor.matmul_mx(
                     out=y_ps[:],
-                    lhsT=w_codes[:, head].bitcast(FP8X4),
-                    lhsT_scale=w_scales[:, head],
+                    lhsT=w_codes[:, tile_cols].bitcast(FP8X4),
+                    lhsT_scale=w_scales[:, tile_cols],
                     rhs=codes[:].bitcast(FP8X4),
                     rhs_scale=scales[:],
                     start=True,
                     stop=True,
                 )
-                proj_tiles[(g, h)] = y_ps
+                proj_tiles[(g, e)] = y_ps
 
-        def rope_products(g, h):
+        def rope_products(g, e):
             cols = slice((g % 2) * GROUP_TOKENS, (g % 2 + 1) * GROUP_TOKENS)
-            y_ps = proj_tiles[(g, h)]
             own = products.tile([P, GROUP_TOKENS], F32)
             nc.vector.scalar_tensor_tensor(
-                out=own[:], in0=y_ps[:], scalar=bias[:, h : h + 1], in1=cos_t[:, cols], op0=ALU.add, op1=ALU.mult
+                out=own[:], in0=proj_tiles[(g, e)][:], scalar=bias[:, e : e + 1], in1=cos_t[:, cols, e], op0=ALU.add, op1=ALU.mult
             )
             lent = products.tile([P, GROUP_TOKENS], F32)
             nc.vector.scalar_tensor_tensor(
-                out=lent[:], in0=y_ps[:], scalar=bias[:, h : h + 1], in1=sin_lent_t[:, cols], op0=ALU.add, op1=ALU.mult
+                out=lent[:], in0=proj_tiles[(g, 1 - e)][:], scalar=bias[:, 1 - e : 2 - e], in1=sin_t[:, cols, e], op0=ALU.add, op1=ALU.mult
             )
-            product_tiles[(g, h)] = (own, lent)
+            product_tiles[(g, e)] = [own, lent]
 
-        def turn_back(g, h, rows, by_product=False):
-            if rows[0] == 0:
-                rope_tile = psum_rope.tile([P, GROUP_ROWS, D], F32, tag="rope")
-                rope_tiles[(g, h)] = rope_tile
-            rope_ps = rope_tiles[(g, h)]
-            own, lent = product_tiles[(g, h)]
-            turn = not by_product
-            for j in rows:
-                block = slice(j * P, (j + 1) * P)
-                nc.tensor.matmul(rope_ps[:, j, :], lhsT=own[:, block], rhs=ident_f32[:], is_transpose=turn, start=True, stop=False)
-                nc.tensor.matmul(rope_ps[:, j, :], lhsT=lent[:, block], rhs=swap_f32[:], is_transpose=turn, start=False, stop=True)
+        def add_products(g, e):
+            own, lent = product_tiles[(g, e)]
+            rope_sum = products.tile([P, GROUP_TOKENS], F32)
+            nc.gpsimd.tensor_tensor(out=rope_sum[:], in0=own[:], in1=lent[:], op=ALU.add)
+            product_tiles[(g, e)] = [rope_sum]
 
-        def emit(g, h):
-            rope_ps = rope_tiles[(g, h)]
-            out_sb = results.tile([P, GROUP_ROWS, D], F32)
-            nc.scalar.activation(out=out_sb[:], in_=rope_ps[:], func=ACT.Relu)
-            rows = slice((g % 2) * GROUP_ROWS, (g % 2 + 1) * GROUP_ROWS)
-            nc.sync.dma_start(out=out[g // 2, h].rearrange("(p j) d -> p j d", j=ROWS)[:, rows, :], in_=out_sb[:])
+        def turn_back(g, j, by_product=()):
+            if j % 2 == 0:
+                rope_tile = psum_rope.tile([P, 2, 2, P], F32, tag="rope")
+                rope_tiles[(g, j // 2)] = rope_tile
+            rope_ps = rope_tiles[(g, j // 2)]
+            block = slice(j * P, (j + 1) * P)
+            for e in range(2):
+                parts = product_tiles[(g, e)]
+                for n, part in enumerate(parts):
+                    nc.tensor.matmul(
+                        rope_ps[:, j % 2, e, :],
+                        lhsT=part[:, block],
+                        rhs=ident_f32[:],
+                        is_transpose=(e, n) not in by_product,
+                        start=n == 0,
+                        stop=n == len(parts) - 1,
+                    )
 
-        def table_to_channels(table_sb, table_t):
-            table_ps = psum_proj.tile([P, ROWS, P], BF16, tag="proj")
-            for j in range(ROWS):
-                nc.tensor.transpose(table_ps[:, j, :], table_sb[:, j, :], ident_bf16[:])
-            nc.scalar.copy(out=table_t[:], in_=table_ps[:].rearrange("d j p -> d (j p)"))
+        def emit(g, half):
+            if half == 0:
+                result_tile = results.tile([P, H, GROUP_ROWS, D], F32)
+                result_tiles[g] = result_tile
+            out_sb = result_tiles[g]
+            rope_ps = rope_tiles[(g, half)]
+            for h in range(H):
+                nc.scalar.activation(
+                    out=out_sb[:, h, 2 * half : 2 * half + 2, :].rearrange("p j (i e) -> p j i e", e=2),
+                    in_=rope_ps[:, :, :, h * PAIRS : (h + 1) * PAIRS].rearrange("p j e i -> p j i e"),
+                    func=ACT.Relu,
+                )
+            if half == 1:
+                rows = slice((g % 2) * GROUP_ROWS, (g % 2 + 1) * GROUP_ROWS)
+                nc.sync.dma_start(out=out[g // 2].rearrange("h (p j) d -> p h j d", j=ROWS)[:, :, rows, :], in_=out_sb[:])
 
-        turn_tokens(0)
-        cos_t = const.tile([P, S], BF16)
-        table_to_channels(cos_sb, cos_t)
-        turn_tokens(1)
+        def table_to_channels(doubled, table_t, copy):
+            table_words = table_t[:].rearrange("q s e -> q (s e)").bitcast(F32)
+            for half in range(2):
+                table_ps = psum_proj.tile([P, GROUP_ROWS, P], F32, tag="proj")
+                for j in range(GROUP_ROWS):
+                    nc.tensor.transpose(table_ps[:, j, :], doubled[:, half * GROUP_ROWS + j, :], ident_f32[:])
+                copy(out=table_words[:, half * GROUP_TOKENS : (half + 1) * GROUP_TOKENS], in_=table_ps[:].rearrange("q j p -> q (j p)"))
+
+        turn_half(0, 0)
+        turn_half(0, 1)
         quantise(0)
         project(0)
-        sin_lent = const.tile([P, ROWS, D], BF16)
-        sin_pairs = sin_sb[:].rearrange("p j (i two) -> p j i two", two=2)
-        lent_pairs = sin_lent[:].rearrange("p j (i two) -> p j i two", two=2)
-        nc.gpsimd.tensor_scalar(out=lent_pairs[:, :, :, 0], in0=sin_pairs[:, :, :, 1], scalar1=1.0, scalar2=0.0, op0=ALU.mult, op1=ALU.add)
-        nc.gpsimd.tensor_scalar(out=lent_pairs[:, :, :, 1], in0=sin_pairs[:, :, :, 0], scalar1=-1.0, scalar2=0.0, op0=ALU.mult, op1=ALU.add)
-        sin_lent_t = const.tile([P, S], BF16)
-        table_to_channels(sin_lent, sin_lent_t)
-        turn_tokens(2)
-        quantise(1)
-        project(1)
 
-        for g in range(GROUPS):
-            rope_products(g, 0)
+        bias_ps = psum_rope.tile([P, P], F32, tag="rope")
+        nc.tensor.transpose(bias_ps[:], bias_row[:].bitcast(F32), ident_f32[:])
+        bias_pair = const.tile([P, 2], BF16)
+        nc.vector.tensor_copy(out=bias_pair[:].bitcast(F32), in_=bias_ps[:, 0:1])
+        bias = const.tile([P, 2], F32)
+        nc.vector.tensor_copy(out=bias[:], in_=bias_pair[:])
+
+        cos_doubled = const.tile([P, ROWS, H, D], BF16)
+        for h in range(H):
+            nc.vector.tensor_copy(out=cos_doubled[:, :, h, :].bitcast(F32), in_=cos_sb[:].bitcast(F32))
+        cos_t = const.tile([P, S, 2], BF16)
+        table_to_channels(cos_doubled[:].rearrange("p j h d -> p j (h d)").bitcast(F32), cos_t, nc.scalar.copy)
+
+        turn_half(1, 0)
+        turn_half(1, 1)
+        quantise(1)
+
+        sin_doubled = const.tile([P, ROWS, H, D], BF16)
+        sin_pairs = sin_sb[:].rearrange("p j (i e) -> p j i e", e=2)
+        for h in range(H):
+            doubled_pairs = sin_doubled[:, :, h, :].rearrange("p j (i e) -> p j i e", e=2)
+            for e in range(2):
+                nc.gpsimd.tensor_scalar(
+                    out=doubled_pairs[:, :, :, e], in0=sin_pairs[:, :, :, e], scalar1=2.0 * e - 1.0, scalar2=0.0, op0=ALU.mult, op1=ALU.add
+                )
+        sin_t = const.tile([P, S, 2], BF16)
+        table_to_channels(sin_doubled[:].rearrange("p j h d -> p j (h d)").bitcast(F32), sin_t, nc.vector.tensor_copy)
+
+        turn_half(2, 0)
+        turn_half(2, 1)
+
+        for g in range(GROUPS + 1):
+            if g + 1 < GROUPS:
+                project(g + 1)
+            if g < GROUPS:
+                rope_products(g, 0)
+                add_products(g, 0)
             if g >= 1:
-                turn_back(g - 1, 1, [0, 1, 2])
+                turn_back(g - 1, 0)
+                turn_back(g - 1, 1)
+                emit(g - 1, 0)
             if g + 3 < GROUPS:
                 turn_half(g + 3, 0)
+            if g < GROUPS:
+                rope_products(g, 1)
             if g >= 1:
-                turn_back(g - 1, 1, [3], by_product=True)
-                emit(g - 1, 1)
+                turn_back(g - 1, 2, by_product=[(0, 0), (1, 0)])
             if g + 3 < GROUPS:
                 turn_half(g + 3, 1)
+            if g >= 1:
+                turn_back(g - 1, 3)
+                emit(g - 1, 1)
             if g + 2 < GROUPS:
                 quantise(g + 2)
-            turn_back(g, 0, [0, 1, 2, 3])
-            emit(g, 0)
-            if g + 2 < GROUPS:
-                project(g + 2)
-            rope_products(g, 1)
-        turn_back(GROUPS - 1, 1, [0, 1, 2, 3])
-        emit(GROUPS - 1, 1)

@@ -19,6 +19,7 @@ ROWS = S // P
 GROUP_ROWS = 4
 GROUP_TOKENS = GROUP_ROWS * P
 GROUPS = B * ROWS // GROUP_ROWS
+AHEAD = 3
 
 FLOPS = 2 * B * S * C * H * D
 
@@ -28,12 +29,12 @@ def tile_lineartransformerblock_pa_t_kernel(tc, x, cos, sin, Wq, bq, out):
     with ExitStack() as ctx:
         const = ctx.enter_context(tc.tile_pool(name="const", bufs=1))
         tokens = ctx.enter_context(tc.tile_pool(name="tokens", bufs=GROUPS))
-        staged = ctx.enter_context(tc.tile_pool(name="staged", bufs=3))
-        products = ctx.enter_context(tc.tile_pool(name="products", bufs=3))
-        results = ctx.enter_context(tc.tile_pool(name="results", bufs=4))
-        psum_words = ctx.enter_context(tc.psum_pool(name="psum_words", bufs=2))
-        psum_proj = ctx.enter_context(tc.psum_pool(name="psum_proj", bufs=4))
-        psum_rope = ctx.enter_context(tc.psum_pool(name="psum_rope", bufs=2))
+        staged = ctx.enter_context(tc.tile_pool(name="staged", bufs=1))
+        products = ctx.enter_context(tc.tile_pool(name="products", bufs=1))
+        results = ctx.enter_context(tc.tile_pool(name="results", bufs=1))
+        psum_words = ctx.enter_context(tc.psum_pool(name="psum_words", bufs=1))
+        psum_proj = ctx.enter_context(tc.psum_pool(name="psum_proj", bufs=1))
+        psum_rope = ctx.enter_context(tc.psum_pool(name="psum_rope", bufs=1))
         ctx.enter_context(tc.manual_schedule())
 
         ident_f32 = const.tile([P, P], F32)
@@ -41,6 +42,7 @@ def tile_lineartransformerblock_pa_t_kernel(tc, x, cos, sin, Wq, bq, out):
         bias_row = const.tile([P, H * D], BF16)
         nc.vector.memset(bias_row[:], 0.0)
 
+        nc.sync.dma_start(out=bias_row[0:1, :], in_=bq.rearrange("(o c) -> o c", o=1))
         w_sb = const.tile([P, 2, C], BF16)
         nc.sync.dma_start(out=w_sb[:], in_=Wq.rearrange("(q e) k -> q e k", e=2))
 
@@ -53,7 +55,6 @@ def tile_lineartransformerblock_pa_t_kernel(tc, x, cos, sin, Wq, bq, out):
             x_tiles[g] = x_sb
 
         load_tokens(0)
-        nc.sync.dma_start(out=bias_row[0:1, :], in_=bq.rearrange("(o c) -> o c", o=1))
         cos_sb = const.tile([P, ROWS, D], BF16)
         nc.sync.dma_start(out=cos_sb[:], in_=cos.rearrange("(p j) d -> p j d", j=ROWS))
         sin_sb = const.tile([P, ROWS, D], BF16)
@@ -61,8 +62,8 @@ def tile_lineartransformerblock_pa_t_kernel(tc, x, cos, sin, Wq, bq, out):
         for g in range(1, GROUPS):
             load_tokens(g)
 
-        def words_to_partitions(row_blocks, grouped_words):
-            words_ps = psum_words.tile([P, 2, 2 * P], F32, tag="words")
+        def words_to_partitions(row_blocks, grouped_words, half):
+            words_ps = psum_words.tile([P, 2, 2 * P], F32, tag="words%d" % half)
             for r, block in enumerate(row_blocks):
                 for u in range(2):
                     nc.tensor.transpose(words_ps[:, u, r * P : (r + 1) * P], block[:, u::2], ident_f32[:])
@@ -72,6 +73,7 @@ def tile_lineartransformerblock_pa_t_kernel(tc, x, cos, sin, Wq, bq, out):
         words_to_partitions(
             [w_sb[:, e, :].bitcast(F32) for e in range(2)],
             w_grouped[:].bitcast(F32).rearrange("p (c u) -> p c u", u=2),
+            1,
         )
         w_codes = const.tile([P, 2 * P], U32, align_bytes=64)
         w_scales = const.tile([P, 2 * P], U8, align_bytes=64)
@@ -86,17 +88,18 @@ def tile_lineartransformerblock_pa_t_kernel(tc, x, cos, sin, Wq, bq, out):
 
         def turn_half(g, half):
             if half == 0:
-                grouped_tile = staged.tile([P, GROUP_TOKENS * PACK], BF16, align_bytes=64)
+                grouped_tile = staged.tile([P, GROUP_TOKENS * PACK], BF16, align_bytes=64, tag="grouped%d" % (g % AHEAD))
                 grouped_tiles[g] = grouped_tile
             grouped_words = grouped_tiles[g][:].bitcast(F32).rearrange("p (c u) -> p c u", u=2)
             words_to_partitions(
                 [x_tiles[g][:, 2 * half + r, :].bitcast(F32) for r in range(2)],
                 grouped_words[:, half * 2 * P : (half + 1) * 2 * P, :],
+                half,
             )
 
         def quantise(g):
-            codes = staged.tile([P, GROUP_TOKENS], U32, align_bytes=64)
-            scales = staged.tile([P, GROUP_TOKENS], U8, align_bytes=64)
+            codes = staged.tile([P, GROUP_TOKENS], U32, align_bytes=64, tag="codes%d" % (g % AHEAD))
+            scales = staged.tile([P, GROUP_TOKENS], U8, align_bytes=64, tag="scales%d" % (g % AHEAD))
             nc.vector.quantize_mx(out=codes[:].bitcast(FP8X4), scales=scales[:], in_=grouped_tiles[g][:])
             code_tiles[g] = (codes, scales)
 
@@ -104,7 +107,7 @@ def tile_lineartransformerblock_pa_t_kernel(tc, x, cos, sin, Wq, bq, out):
             codes, scales = code_tiles[g]
             for e in range(2):
                 tile_cols = slice(e * P, (e + 1) * P)
-                y_ps = psum_proj.tile([P, GROUP_TOKENS], F32, tag="proj")
+                y_ps = psum_proj.tile([P, GROUP_TOKENS], F32, tag="proj%d%d" % (g % 2, e))
                 nc.tensor.matmul_mx(
                     out=y_ps[:],
                     lhsT=w_codes[:, tile_cols].bitcast(FP8X4),
@@ -118,11 +121,11 @@ def tile_lineartransformerblock_pa_t_kernel(tc, x, cos, sin, Wq, bq, out):
 
         def rope_products(g, e):
             cols = slice((g % 2) * GROUP_TOKENS, (g % 2 + 1) * GROUP_TOKENS)
-            own = products.tile([P, GROUP_TOKENS], F32)
+            own = products.tile([P, GROUP_TOKENS], F32, tag="own%d%d" % (g % AHEAD, e))
             nc.vector.scalar_tensor_tensor(
                 out=own[:], in0=proj_tiles[(g, e)][:], scalar=bias[:, e : e + 1], in1=cos_t[:, cols, e], op0=ALU.add, op1=ALU.mult
             )
-            lent = products.tile([P, GROUP_TOKENS], F32)
+            lent = products.tile([P, GROUP_TOKENS], F32, tag="lent%d%d" % (g % AHEAD, e))
             nc.vector.scalar_tensor_tensor(
                 out=lent[:], in0=proj_tiles[(g, 1 - e)][:], scalar=bias[:, 1 - e : 2 - e], in1=sin_t[:, cols, e], op0=ALU.add, op1=ALU.mult
             )
@@ -130,13 +133,13 @@ def tile_lineartransformerblock_pa_t_kernel(tc, x, cos, sin, Wq, bq, out):
 
         def add_products(g, e):
             own, lent = product_tiles[(g, e)]
-            rope_sum = products.tile([P, GROUP_TOKENS], F32)
-            nc.gpsimd.tensor_tensor(out=rope_sum[:], in0=own[:], in1=lent[:], op=ALU.add)
+            rope_sum = products.tile([P, GROUP_TOKENS], F32, tag="sum%d%d" % (g % AHEAD, e))
+            nc.gpsimd.tensor_tensor(out=rope_sum[:], in0=own[:], in1=lent[:], op=ALU.subtract)
             product_tiles[(g, e)] = [rope_sum]
 
         def turn_back(g, j, by_product=()):
             if j % 2 == 0:
-                rope_tile = psum_rope.tile([P, 2, 2, P], F32, tag="rope")
+                rope_tile = psum_rope.tile([P, 2, 2, P], F32, tag="rope%d" % (j // 2))
                 rope_tiles[(g, j // 2)] = rope_tile
             rope_ps = rope_tiles[(g, j // 2)]
             block = slice(j * P, (j + 1) * P)
@@ -154,7 +157,7 @@ def tile_lineartransformerblock_pa_t_kernel(tc, x, cos, sin, Wq, bq, out):
 
         def emit(g, half):
             if half == 0:
-                result_tile = results.tile([P, H, GROUP_ROWS, D], F32)
+                result_tile = results.tile([P, H, GROUP_ROWS, D], F32, tag="result%d" % (g % 4))
                 result_tiles[g] = result_tile
             out_sb = result_tiles[g]
             rope_ps = rope_tiles[(g, half)]
@@ -168,47 +171,42 @@ def tile_lineartransformerblock_pa_t_kernel(tc, x, cos, sin, Wq, bq, out):
                 rows = slice((g % 2) * GROUP_ROWS, (g % 2 + 1) * GROUP_ROWS)
                 nc.sync.dma_start(out=out[g // 2].rearrange("h (p j) d -> p h j d", j=ROWS)[:, :, rows, :], in_=out_sb[:])
 
-        def table_to_channels(doubled, table_t, copy):
-            table_words = table_t[:].rearrange("q s e -> q (s e)").bitcast(F32)
-            for half in range(2):
-                table_ps = psum_proj.tile([P, GROUP_ROWS, P], F32, tag="proj")
-                for j in range(GROUP_ROWS):
-                    nc.tensor.transpose(table_ps[:, j, :], doubled[:, half * GROUP_ROWS + j, :], ident_f32[:])
-                copy(out=table_words[:, half * GROUP_TOKENS : (half + 1) * GROUP_TOKENS], in_=table_ps[:].rearrange("q j p -> q (j p)"))
-
-        turn_half(0, 0)
-        turn_half(0, 1)
-        quantise(0)
-        project(0)
-
-        bias_ps = psum_rope.tile([P, P], F32, tag="rope")
+        bias_ps = psum_rope.tile([P, P], F32, tag="rope0")
         nc.tensor.transpose(bias_ps[:], bias_row[:].bitcast(F32), ident_f32[:])
         bias_pair = const.tile([P, 2], BF16)
         nc.vector.tensor_copy(out=bias_pair[:].bitcast(F32), in_=bias_ps[:, 0:1])
         bias = const.tile([P, 2], F32)
         nc.vector.tensor_copy(out=bias[:], in_=bias_pair[:])
 
-        cos_doubled = const.tile([P, ROWS, H, D], BF16)
-        for h in range(H):
-            nc.vector.tensor_copy(out=cos_doubled[:, :, h, :].bitcast(F32), in_=cos_sb[:].bitcast(F32))
-        cos_t = const.tile([P, S, 2], BF16)
-        table_to_channels(cos_doubled[:].rearrange("p j h d -> p j (h d)").bitcast(F32), cos_t, nc.scalar.copy)
+        def double_table(table_sb, doubled):
+            for h in range(H):
+                nc.vector.tensor_copy(out=doubled[:, :, h, :].bitcast(F32), in_=table_sb[:].bitcast(F32))
 
+        def table_to_channels(doubled, table_t, pool, tag, copy):
+            words = doubled[:].rearrange("p j h d -> p j (h d)").bitcast(F32)
+            table_words = table_t[:].rearrange("q s e -> q (s e)").bitcast(F32)
+            for half in range(2):
+                table_ps = pool.tile([P, GROUP_ROWS, P], F32, tag="%s%d" % (tag, half))
+                for j in range(GROUP_ROWS):
+                    nc.tensor.transpose(table_ps[:, j, :], words[:, half * GROUP_ROWS + j, :], ident_f32[:])
+                copy(out=table_words[:, half * GROUP_TOKENS : (half + 1) * GROUP_TOKENS], in_=table_ps[:].rearrange("q j p -> q (j p)"))
+
+        cos_doubled = const.tile([P, ROWS, H, D], BF16)
+        sin_doubled = const.tile([P, ROWS, H, D], BF16)
+        cos_t = const.tile([P, S, 2], BF16)
+        sin_t = const.tile([P, S, 2], BF16)
+
+        turn_half(0, 0)
+        turn_half(0, 1)
+        double_table(cos_sb, cos_doubled)
+        table_to_channels(cos_doubled, cos_t, psum_proj, "proj1", nc.scalar.copy)
+        quantise(0)
+        project(0)
+        double_table(sin_sb, sin_doubled)
         turn_half(1, 0)
         turn_half(1, 1)
+        table_to_channels(sin_doubled, sin_t, psum_rope, "rope", nc.vector.tensor_copy)
         quantise(1)
-
-        sin_doubled = const.tile([P, ROWS, H, D], BF16)
-        sin_pairs = sin_sb[:].rearrange("p j (i e) -> p j i e", e=2)
-        for h in range(H):
-            doubled_pairs = sin_doubled[:, :, h, :].rearrange("p j (i e) -> p j i e", e=2)
-            for e in range(2):
-                nc.gpsimd.tensor_scalar(
-                    out=doubled_pairs[:, :, :, e], in0=sin_pairs[:, :, :, e], scalar1=2.0 * e - 1.0, scalar2=0.0, op0=ALU.mult, op1=ALU.add
-                )
-        sin_t = const.tile([P, S, 2], BF16)
-        table_to_channels(sin_doubled[:].rearrange("p j h d -> p j (h d)").bitcast(F32), sin_t, nc.vector.tensor_copy)
-
         turn_half(2, 0)
         turn_half(2, 1)
 

@@ -19,7 +19,8 @@ ROWS = S // P
 GROUP_ROWS = 4
 GROUP_TOKENS = GROUP_ROWS * P
 GROUPS = B * ROWS // GROUP_ROWS
-AHEAD = 3
+AHEAD = 4
+COPIES = 3
 
 FLOPS = 2 * B * S * C * H * D
 
@@ -42,64 +43,78 @@ def tile_lineartransformerblock_pa_t_kernel(tc, x, cos, sin, Wq, bq, out):
         bias_row = const.tile([P, H * D], BF16)
         nc.vector.memset(bias_row[:], 0.0)
 
-        nc.sync.dma_start(out=bias_row[0:1, :], in_=bq.rearrange("(o c) -> o c", o=1))
-        w_sb = const.tile([P, 2, C], BF16)
-        nc.sync.dma_start(out=w_sb[:], in_=Wq.rearrange("(q e) k -> q e k", e=2))
-
         x_tiles = {}
 
-        def load_tokens(g):
-            rows = slice((g % 2) * GROUP_ROWS, (g % 2 + 1) * GROUP_ROWS)
+        def load_tokens(g, parts=1):
             x_sb = tokens.tile([P, GROUP_ROWS, C], BF16)
-            nc.sync.dma_start(out=x_sb[:], in_=x[g // 2].rearrange("(p j) k -> p j k", j=ROWS)[:, rows, :])
+            first_row = (g % 2) * GROUP_ROWS
+            step = GROUP_ROWS // parts
+            for r in range(0, GROUP_ROWS, step):
+                nc.sync.dma_start(
+                    out=x_sb[:, r : r + step, :],
+                    in_=x[g // 2].rearrange("(p j) k -> p j k", j=ROWS)[:, first_row + r : first_row + r + step, :],
+                )
             x_tiles[g] = x_sb
 
-        load_tokens(0)
+        load_tokens(0, parts=2)
+        w_sb = const.tile([P, 2, C], BF16)
+        nc.sync.dma_start(out=w_sb[:], in_=Wq.rearrange("(q e) k -> q e k", e=2))
         cos_sb = const.tile([P, ROWS, D], BF16)
         nc.sync.dma_start(out=cos_sb[:], in_=cos.rearrange("(p j) d -> p j d", j=ROWS))
+        nc.sync.dma_start(out=bias_row[0:1, :], in_=bq.rearrange("(o c) -> o c", o=1))
         sin_sb = const.tile([P, ROWS, D], BF16)
         nc.sync.dma_start(out=sin_sb[:], in_=sin.rearrange("(p j) d -> p j d", j=ROWS))
         for g in range(1, GROUPS):
             load_tokens(g)
 
-        def words_to_partitions(row_blocks, grouped_words, half):
-            words_ps = psum_words.tile([P, 2, 2 * P], F32, tag="words%d" % half)
+        def words_to_partitions(row_blocks, grouped_words, pool, tag, copy):
+            words_ps = pool.tile([P, 2, 2 * P], F32, tag=tag)
             for r, block in enumerate(row_blocks):
                 for u in range(2):
                     nc.tensor.transpose(words_ps[:, u, r * P : (r + 1) * P], block[:, u::2], ident_f32[:])
-            nc.scalar.copy(out=grouped_words, in_=words_ps[:].rearrange("p u c -> p c u"))
+            copy(out=grouped_words, in_=words_ps[:].rearrange("p u c -> p c u"))
 
         w_grouped = const.tile([P, 2 * P * PACK], BF16, align_bytes=64)
-        words_to_partitions(
-            [w_sb[:, e, :].bitcast(F32) for e in range(2)],
-            w_grouped[:].bitcast(F32).rearrange("p (c u) -> p c u", u=2),
-            1,
-        )
         w_codes = const.tile([P, 2 * P], U32, align_bytes=64)
         w_scales = const.tile([P, 2 * P], U8, align_bytes=64)
-        nc.vector.quantize_mx(out=w_codes[:].bitcast(FP8X4), scales=w_scales[:], in_=w_grouped[:])
+
+        def turn_weights():
+            words_to_partitions(
+                [w_sb[:, e, :].bitcast(F32) for e in range(2)],
+                w_grouped[:].bitcast(F32).rearrange("p (c u) -> p c u", u=2),
+                psum_proj,
+                "proj10",
+                nc.vector.tensor_copy,
+            )
 
         grouped_tiles = {}
         code_tiles = {}
         proj_tiles = {}
         product_tiles = {}
+        even_sums = {}
         rope_tiles = {}
         result_tiles = {}
 
         def turn_half(g, half):
             if half == 0:
-                grouped_tile = staged.tile([P, GROUP_TOKENS * PACK], BF16, align_bytes=64, tag="grouped%d" % (g % AHEAD))
+                grouped_tile = staged.tile([P, GROUP_TOKENS * PACK], BF16, align_bytes=64, tag="grouped%d" % (g % (AHEAD + 1)))
                 grouped_tiles[g] = grouped_tile
             grouped_words = grouped_tiles[g][:].bitcast(F32).rearrange("p (c u) -> p c u", u=2)
             words_to_partitions(
                 [x_tiles[g][:, 2 * half + r, :].bitcast(F32) for r in range(2)],
                 grouped_words[:, half * 2 * P : (half + 1) * 2 * P, :],
-                half,
+                psum_words,
+                "words%d" % half,
+                nc.scalar.copy,
             )
 
+        def turn_group(g):
+            for half in range(2):
+                turn_half(g, half)
+
         def quantise(g):
-            codes = staged.tile([P, GROUP_TOKENS], U32, align_bytes=64, tag="codes%d" % (g % AHEAD))
-            scales = staged.tile([P, GROUP_TOKENS], U8, align_bytes=64, tag="scales%d" % (g % AHEAD))
+            codes = staged.tile([P, GROUP_TOKENS], U32, align_bytes=64, tag="codes%d" % (g % COPIES))
+            scales = staged.tile([P, GROUP_TOKENS], U8, align_bytes=64, tag="scales%d" % (g % COPIES))
             nc.vector.quantize_mx(out=codes[:].bitcast(FP8X4), scales=scales[:], in_=grouped_tiles[g][:])
             code_tiles[g] = (codes, scales)
 
@@ -119,23 +134,30 @@ def tile_lineartransformerblock_pa_t_kernel(tc, x, cos, sin, Wq, bq, out):
                 )
                 proj_tiles[(g, e)] = y_ps
 
-        def rope_products(g, e):
-            cols = slice((g % 2) * GROUP_TOKENS, (g % 2 + 1) * GROUP_TOKENS)
-            own = products.tile([P, GROUP_TOKENS], F32, tag="own%d%d" % (g % AHEAD, e))
-            nc.vector.scalar_tensor_tensor(
-                out=own[:], in0=proj_tiles[(g, e)][:], scalar=bias[:, e : e + 1], in1=cos_t[:, cols, e], op0=ALU.add, op1=ALU.mult
-            )
-            lent = products.tile([P, GROUP_TOKENS], F32, tag="lent%d%d" % (g % AHEAD, e))
-            nc.vector.scalar_tensor_tensor(
-                out=lent[:], in0=proj_tiles[(g, 1 - e)][:], scalar=bias[:, 1 - e : 2 - e], in1=sin_t[:, cols, e], op0=ALU.add, op1=ALU.mult
-            )
-            product_tiles[(g, e)] = [own, lent]
-
-        def add_products(g, e):
+        def rope_products(g, e, cols):
+            if cols.start == 0:
+                own_tile = products.tile([P, GROUP_TOKENS], F32, tag="own%d%d" % (g % COPIES, e))
+                lent_tile = products.tile([P, GROUP_TOKENS], F32, tag="lent%d%d" % (g % COPIES, e))
+                product_tiles[(g, e)] = [own_tile, lent_tile]
             own, lent = product_tiles[(g, e)]
-            rope_sum = products.tile([P, GROUP_TOKENS], F32, tag="sum%d%d" % (g % AHEAD, e))
-            nc.gpsimd.tensor_tensor(out=rope_sum[:], in0=own[:], in1=lent[:], op=ALU.subtract)
-            product_tiles[(g, e)] = [rope_sum]
+            first = (g % 2) * GROUP_TOKENS
+            table_cols = slice(first + cols.start, first + cols.stop)
+            for part, y_parity, table in ((own, e, cos_t), (lent, 1 - e, sin_t)):
+                nc.vector.scalar_tensor_tensor(
+                    out=part[:, cols],
+                    in0=proj_tiles[(g, y_parity)][:, cols],
+                    scalar=bias[:, y_parity : y_parity + 1],
+                    in1=table[:, table_cols, e],
+                    op0=ALU.add,
+                    op1=ALU.mult,
+                )
+
+        def subtract_products(g, cols):
+            own, lent = product_tiles[(g, 0)]
+            if cols.start == 0:
+                sum_tile = products.tile([P, GROUP_TOKENS], F32, tag="sum%d" % (g % COPIES))
+                even_sums[g] = sum_tile
+            nc.gpsimd.tensor_tensor(out=even_sums[g][:, cols], in0=own[:, cols], in1=lent[:, cols], op=ALU.subtract)
 
         def turn_back(g, j, by_product=()):
             if j % 2 == 0:
@@ -144,7 +166,7 @@ def tile_lineartransformerblock_pa_t_kernel(tc, x, cos, sin, Wq, bq, out):
             rope_ps = rope_tiles[(g, j // 2)]
             block = slice(j * P, (j + 1) * P)
             for e in range(2):
-                parts = product_tiles[(g, e)]
+                parts = product_tiles[(g, 1)] if e == 1 else [even_sums[g]]
                 for n, part in enumerate(parts):
                     nc.tensor.matmul(
                         rope_ps[:, j % 2, e, :],
@@ -156,40 +178,37 @@ def tile_lineartransformerblock_pa_t_kernel(tc, x, cos, sin, Wq, bq, out):
                     )
 
         def emit(g, half):
-            if half == 0:
-                result_tile = results.tile([P, H, GROUP_ROWS, D], F32, tag="result%d" % (g % 4))
+            by_half = g == GROUPS - 1
+            tile_rows = 2 if by_half else GROUP_ROWS
+            if half == 0 or by_half:
+                result_tile = results.tile([P, H, tile_rows, D], F32, tag="result%d" % ((g + half if by_half else g) % 4))
                 result_tiles[g] = result_tile
             out_sb = result_tiles[g]
+            first = 0 if by_half else 2 * half
             rope_ps = rope_tiles[(g, half)]
             for h in range(H):
                 nc.scalar.activation(
-                    out=out_sb[:, h, 2 * half : 2 * half + 2, :].rearrange("p j (i e) -> p j i e", e=2),
+                    out=out_sb[:, h, first : first + 2, :].rearrange("p j (i e) -> p j i e", e=2),
                     in_=rope_ps[:, :, :, h * PAIRS : (h + 1) * PAIRS].rearrange("p j e i -> p j i e"),
                     func=ACT.Relu,
                 )
-            if half == 1:
-                rows = slice((g % 2) * GROUP_ROWS, (g % 2 + 1) * GROUP_ROWS)
-                nc.sync.dma_start(out=out[g // 2].rearrange("h (p j) d -> p h j d", j=ROWS)[:, :, rows, :], in_=out_sb[:])
-
-        bias_ps = psum_rope.tile([P, P], F32, tag="rope0")
-        nc.tensor.transpose(bias_ps[:], bias_row[:].bitcast(F32), ident_f32[:])
-        bias_pair = const.tile([P, 2], BF16)
-        nc.vector.tensor_copy(out=bias_pair[:].bitcast(F32), in_=bias_ps[:, 0:1])
-        bias = const.tile([P, 2], F32)
-        nc.vector.tensor_copy(out=bias[:], in_=bias_pair[:])
+            if half == 1 or by_half:
+                first_row = (g % 2) * GROUP_ROWS + (2 * half if by_half else 0)
+                nc.sync.dma_start(
+                    out=out[g // 2].rearrange("h (p j) d -> p h j d", j=ROWS)[:, :, first_row : first_row + tile_rows, :], in_=out_sb[:]
+                )
 
         def double_table(table_sb, doubled):
             for h in range(H):
                 nc.vector.tensor_copy(out=doubled[:, :, h, :].bitcast(F32), in_=table_sb[:].bitcast(F32))
 
-        def table_to_channels(doubled, table_t, pool, tag, copy):
+        def table_to_channels(doubled, table_t, half, tag):
             words = doubled[:].rearrange("p j h d -> p j (h d)").bitcast(F32)
             table_words = table_t[:].rearrange("q s e -> q (s e)").bitcast(F32)
-            for half in range(2):
-                table_ps = pool.tile([P, GROUP_ROWS, P], F32, tag="%s%d" % (tag, half))
-                for j in range(GROUP_ROWS):
-                    nc.tensor.transpose(table_ps[:, j, :], words[:, half * GROUP_ROWS + j, :], ident_f32[:])
-                copy(out=table_words[:, half * GROUP_TOKENS : (half + 1) * GROUP_TOKENS], in_=table_ps[:].rearrange("q j p -> q (j p)"))
+            table_ps = psum_rope.tile([P, GROUP_ROWS, P], F32, tag=tag)
+            for j in range(GROUP_ROWS):
+                nc.tensor.transpose(table_ps[:, j, :], words[:, half * GROUP_ROWS + j, :], ident_f32[:])
+            nc.scalar.copy(out=table_words[:, half * GROUP_TOKENS : (half + 1) * GROUP_TOKENS], in_=table_ps[:].rearrange("q j p -> q (j p)"))
 
         cos_doubled = const.tile([P, ROWS, H, D], BF16)
         sin_doubled = const.tile([P, ROWS, H, D], BF16)
@@ -199,37 +218,58 @@ def tile_lineartransformerblock_pa_t_kernel(tc, x, cos, sin, Wq, bq, out):
         turn_half(0, 0)
         turn_half(0, 1)
         double_table(cos_sb, cos_doubled)
-        table_to_channels(cos_doubled, cos_t, psum_proj, "proj1", nc.scalar.copy)
-        quantise(0)
-        project(0)
         double_table(sin_sb, sin_doubled)
-        turn_half(1, 0)
-        turn_half(1, 1)
-        table_to_channels(sin_doubled, sin_t, psum_rope, "rope", nc.vector.tensor_copy)
-        quantise(1)
-        turn_half(2, 0)
-        turn_half(2, 1)
+        turn_weights()
+        nc.vector.quantize_mx(out=w_codes[:].bitcast(FP8X4), scales=w_scales[:], in_=w_grouped[:])
+        table_to_channels(cos_doubled, cos_t, 0, "rope0")
+        table_to_channels(sin_doubled, sin_t, 0, "rope1")
+        quantise(0)
 
-        for g in range(GROUPS + 1):
+        bias_ps = psum_proj.tile([P, P], F32, tag="proj11")
+        nc.tensor.transpose(bias_ps[:], bias_row[:].bitcast(F32), ident_f32[:])
+        project(0)
+        bias_pair = const.tile([P, 2], BF16)
+        nc.vector.tensor_copy(out=bias_pair[:].bitcast(F32), in_=bias_ps[:, 0:1])
+        bias = const.tile([P, 2], F32)
+        nc.vector.tensor_copy(out=bias[:], in_=bias_pair[:])
+        turn_group(1)
+        table_to_channels(cos_doubled, cos_t, 1, "rope0")
+        table_to_channels(sin_doubled, sin_t, 1, "rope1")
+
+        whole = slice(0, GROUP_TOKENS)
+        rope_products(0, 0, whole)
+        subtract_products(0, whole)
+        turn_group(2)
+        quantise(1)
+        project(1)
+        rope_products(0, 1, whole)
+        turn_group(3)
+        quantise(2)
+
+        for g in range(1, GROUPS + 1):
+            ahead = g + AHEAD - 1
             if g + 1 < GROUPS:
                 project(g + 1)
-            if g < GROUPS:
-                rope_products(g, 0)
-                add_products(g, 0)
-            if g >= 1:
-                turn_back(g - 1, 0)
-                turn_back(g - 1, 1)
-                emit(g - 1, 0)
-            if g + 3 < GROUPS:
-                turn_half(g + 3, 0)
-            if g < GROUPS:
-                rope_products(g, 1)
-            if g >= 1:
-                turn_back(g - 1, 2, by_product=[(0, 0), (1, 0)])
-            if g + 3 < GROUPS:
-                turn_half(g + 3, 1)
-            if g >= 1:
-                turn_back(g - 1, 3)
-                emit(g - 1, 1)
+            if g < GROUPS - 1:
+                rope_products(g, 0, whole)
+                subtract_products(g, whole)
+            elif g == GROUPS - 1:
+                for half in range(2):
+                    cols = slice(half * 2 * P, (half + 1) * 2 * P)
+                    rope_products(g, 0, cols)
+                    subtract_products(g, cols)
+                    rope_products(g, 1, cols)
             if g + 2 < GROUPS:
                 quantise(g + 2)
+            turn_back(g - 1, 0)
+            turn_back(g - 1, 1)
+            emit(g - 1, 0)
+            if ahead < GROUPS:
+                turn_half(ahead, 0)
+            if g < GROUPS - 1:
+                rope_products(g, 1, whole)
+            turn_back(g - 1, 2, by_product=[(0, 0), (1, 0)])
+            if ahead < GROUPS:
+                turn_half(ahead, 1)
+            turn_back(g - 1, 3)
+            emit(g - 1, 1)

@@ -74,6 +74,11 @@ def tile_lineartransformerblock_pa_t_kernel(tc, x, cos, sin, Wq, bq, out):
                     nc.tensor.transpose(words_ps[:, u, r * P : (r + 1) * P], block[:, u::2], ident_f32[:])
             copy(out=grouped_words, in_=words_ps[:].rearrange("p u c -> p c u"))
 
+        def keep_clock(count, pool, tag):
+            idle_ps = pool.tile([P, P], F32, tag=tag)
+            for n in range(count):
+                nc.tensor.matmul(idle_ps[:], lhsT=ident_f32[:], rhs=ident_f32[:], start=True, stop=True)
+
         w_grouped = const.tile([P, 2 * P * PACK], BF16, align_bytes=64)
         w_codes = const.tile([P, 2 * P], U32, align_bytes=64)
         w_scales = const.tile([P, 2 * P], U8, align_bytes=64)
@@ -215,8 +220,10 @@ def tile_lineartransformerblock_pa_t_kernel(tc, x, cos, sin, Wq, bq, out):
         cos_t = const.tile([P, S, 2], BF16)
         sin_t = const.tile([P, S, 2], BF16)
 
+        keep_clock(4, psum_proj, "proj11")
         turn_half(0, 0)
         turn_half(0, 1)
+        keep_clock(2, psum_proj, "proj11")
         double_table(cos_sb, cos_doubled)
         double_table(sin_sb, sin_doubled)
         turn_weights()
@@ -233,6 +240,7 @@ def tile_lineartransformerblock_pa_t_kernel(tc, x, cos, sin, Wq, bq, out):
         bias = const.tile([P, 2], F32)
         nc.vector.tensor_copy(out=bias[:], in_=bias_pair[:])
         turn_group(1)
+        keep_clock(2, psum_rope, "rope1")
         table_to_channels(cos_doubled, cos_t, 1, "rope0")
         table_to_channels(sin_doubled, sin_t, 1, "rope1")
 

from contextlib import ExitStack

import concourse.mybir as mybir
from concourse.masks import make_identity

F32 = mybir.dt.float32
BF16 = mybir.dt.bfloat16
U32 = mybir.dt.uint32
U8 = mybir.dt.uint8
FP8X4 = mybir.dt.float8_e4m3fn_x4
ALU = mybir.AluOpType
ACT = mybir.ActivationFunctionType

B, S, C, H, D = 8, 1024, 512, 2, 128
P = 128
PACK = 4
PAIRS = D // 2
ROWS = S // P
GROUP_ROWS = 4
GROUP_TOKENS = GROUP_ROWS * P
GROUPS = B * ROWS // GROUP_ROWS
AHEAD = 4
COPIES = 3

FLOPS = 2 * B * S * C * H * D


def tile_lineartransformerblock_pa_t_kernel(tc, x, cos, sin, Wq, bq, out):
    nc = tc.nc
    with ExitStack() as ctx:
        const = ctx.enter_context(tc.tile_pool(name="const", bufs=1))
        tokens = ctx.enter_context(tc.tile_pool(name="tokens", bufs=GROUPS))
        staged = ctx.enter_context(tc.tile_pool(name="staged", bufs=1))
        products = ctx.enter_context(tc.tile_pool(name="products", bufs=1))
        results = ctx.enter_context(tc.tile_pool(name="results", bufs=1))
        psum_words = ctx.enter_context(tc.psum_pool(name="psum_words", bufs=1))
        psum_proj = ctx.enter_context(tc.psum_pool(name="psum_proj", bufs=1))
        psum_rope = ctx.enter_context(tc.psum_pool(name="psum_rope", bufs=1))
        ctx.enter_context(tc.manual_schedule())

        ident_f32 = const.tile([P, P], F32)
        make_identity(nc, ident_f32[:])
        bias_row = const.tile([P, H * D], BF16)
        nc.vector.memset(bias_row[:], 0.0)

        x_tiles = {}

        def load_tokens(g, parts=1):
            x_sb = tokens.tile([P, GROUP_ROWS, C], BF16)
            first_row = (g % 2) * GROUP_ROWS
            step = GROUP_ROWS // parts
            for r in range(0, GROUP_ROWS, step):
                nc.sync.dma_start(
                    out=x_sb[:, r : r + step, :],
                    in_=x[g // 2].rearrange("(p j) k -> p j k", j=ROWS)[:, first_row + r : first_row + r + step, :],
                )
            x_tiles[g] = x_sb

        load_tokens(0, parts=2)
        w_sb = const.tile([P, 2, C], BF16)
        nc.sync.dma_start(out=w_sb[:], in_=Wq.rearrange("(q e) k -> q e k", e=2))
        cos_sb = const.tile([P, ROWS, D], BF16)
        nc.sync.dma_start(out=cos_sb[:], in_=cos.rearrange("(p j) d -> p j d", j=ROWS))
        nc.sync.dma_start(out=bias_row[0:1, :], in_=bq.rearrange("(o c) -> o c", o=1))
        sin_sb = const.tile([P, ROWS, D], BF16)
        nc.sync.dma_start(out=sin_sb[:], in_=sin.rearrange("(p j) d -> p j d", j=ROWS))
        for g in range(1, GROUPS):
            load_tokens(g)

        def words_to_partitions(row_blocks, grouped_words, pool, tag, copy):
            words_ps = pool.tile([P, 2, 2 * P], F32, tag=tag)
            for r, block in enumerate(row_blocks):
                for u in range(2):
                    nc.tensor.transpose(words_ps[:, u, r * P : (r + 1) * P], block[:, u::2], ident_f32[:])
            copy(out=grouped_words, in_=words_ps[:].rearrange("p u c -> p c u"))

        def keep_clock(count, pool, tag):
            idle_ps = pool.tile([P, P], F32, tag=tag)
            for n in range(count):
                nc.tensor.matmul(idle_ps[:], lhsT=ident_f32[:], rhs=ident_f32[:], start=True, stop=True)

        w_grouped = const.tile([P, 2 * P * PACK], BF16, align_bytes=64)
        w_codes = const.tile([P, 2 * P], U32, align_bytes=64)
        w_scales = const.tile([P, 2 * P], U8, align_bytes=64)

        def turn_weights():
            words_to_partitions(
                [w_sb[:, e, :].bitcast(F32) for e in range(2)],
                w_grouped[:].bitcast(F32).rearrange("p (c u) -> p c u", u=2),
                psum_proj,
                "proj10",
                nc.vector.tensor_copy,
            )

        grouped_tiles = {}
        code_tiles = {}
        proj_tiles = {}
        product_tiles = {}
        even_sums = {}
        rope_tiles = {}
        result_tiles = {}

        def turn_half(g, half):
            if half == 0:
                grouped_tile = staged.tile([P, GROUP_TOKENS * PACK], BF16, align_bytes=64, tag="grouped%d" % (g % (AHEAD + 1)))
                grouped_tiles[g] = grouped_tile
            grouped_words = grouped_tiles[g][:].bitcast(F32).rearrange("p (c u) -> p c u", u=2)
            words_to_partitions(
                [x_tiles[g][:, 2 * half + r, :].bitcast(F32) for r in range(2)],
                grouped_words[:, half * 2 * P : (half + 1) * 2 * P, :],
                psum_words,
                "words%d" % half,
                nc.scalar.copy,
            )

        def turn_group(g):
            for half in range(2):
                turn_half(g, half)

        def quantise(g):
            codes = staged.tile([P, GROUP_TOKENS], U32, align_bytes=64, tag="codes%d" % (g % COPIES))
            scales = staged.tile([P, GROUP_TOKENS], U8, align_bytes=64, tag="scales%d" % (g % COPIES))
            nc.vector.quantize_mx(out=codes[:].bitcast(FP8X4), scales=scales[:], in_=grouped_tiles[g][:])
            code_tiles[g] = (codes, scales)

        def project(g):
            codes, scales = code_tiles[g]
            for e in range(2):
                tile_cols = slice(e * P, (e + 1) * P)
                y_ps = psum_proj.tile([P, GROUP_TOKENS], F32, tag="proj%d%d" % (g % 2, e))
                nc.tensor.matmul_mx(
                    out=y_ps[:],
                    lhsT=w_codes[:, tile_cols].bitcast(FP8X4),
                    lhsT_scale=w_scales[:, tile_cols],
                    rhs=codes[:].bitcast(FP8X4),
                    rhs_scale=scales[:],
                    start=True,
                    stop=True,
                )
                proj_tiles[(g, e)] = y_ps

        def rope_products(g, e, cols):
            if cols.start == 0:
                own_tile = products.tile([P, GROUP_TOKENS], F32, tag="own%d%d" % (g % COPIES, e))
                lent_tile = products.tile([P, GROUP_TOKENS], F32, tag="lent%d%d" % (g % COPIES, e))
                product_tiles[(g, e)] = [own_tile, lent_tile]
            own, lent = product_tiles[(g, e)]
            first = (g % 2) * GROUP_TOKENS
            table_cols = slice(first + cols.start, first + cols.stop)
            for part, y_parity, table in ((own, e, cos_t), (lent, 1 - e, sin_t)):
                nc.vector.scalar_tensor_tensor(
                    out=part[:, cols],
                    in0=proj_tiles[(g, y_parity)][:, cols],
                    scalar=bias[:, y_parity : y_parity + 1],
                    in1=table[:, table_cols, e],
                    op0=ALU.add,
                    op1=ALU.mult,
                )

        def subtract_products(g, cols):
            own, lent = product_tiles[(g, 0)]
            if cols.start == 0:
                sum_tile = products.tile([P, GROUP_TOKENS], F32, tag="sum%d" % (g % COPIES))
                even_sums[g] = sum_tile
            nc.gpsimd.tensor_tensor(out=even_sums[g][:, cols], in0=own[:, cols], in1=lent[:, cols], op=ALU.subtract)

        def turn_back(g, j, by_product=()):
            if j % 2 == 0:
                rope_tile = psum_rope.tile([P, 2, 2, P], F32, tag="rope%d" % (j // 2))
                rope_tiles[(g, j // 2)] = rope_tile
            rope_ps = rope_tiles[(g, j // 2)]
            block = slice(j * P, (j + 1) * P)
            for e in range(2):
                parts = product_tiles[(g, 1)] if e == 1 else [even_sums[g]]
                for n, part in enumerate(parts):
                    nc.tensor.matmul(
                        rope_ps[:, j % 2, e, :],
                        lhsT=part[:, block],
                        rhs=ident_f32[:],
                        is_transpose=(e, n) not in by_product,
                        start=n == 0,
                        stop=n == len(parts) - 1,
                    )

        def emit(g, half):
            by_half = g == GROUPS - 1
            tile_rows = 2 if by_half else GROUP_ROWS
            if half == 0 or by_half:
                result_tile = results.tile([P, H, tile_rows, D], F32, tag="result%d" % ((g + half if by_half else g) % 4))
                result_tiles[g] = result_tile
            out_sb = result_tiles[g]
            first = 0 if by_half else 2 * half
            rope_ps = rope_tiles[(g, half)]
            for h in range(H):
                nc.scalar.activation(
                    out=out_sb[:, h, first : first + 2, :].rearrange("p j (i e) -> p j i e", e=2),
                    in_=rope_ps[:, :, :, h * PAIRS : (h + 1) * PAIRS].rearrange("p j e i -> p j i e"),
                    func=ACT.Relu,
                )
            if half == 1 or by_half:
                first_row = (g % 2) * GROUP_ROWS + (2 * half if by_half else 0)
                nc.sync.dma_start(
                    out=out[g // 2].rearrange("h (p j) d -> p h j d", j=ROWS)[:, :, first_row : first_row + tile_rows, :], in_=out_sb[:]
                )

        def double_table(table_sb, doubled):
            for h in range(H):
                nc.vector.tensor_copy(out=doubled[:, :, h, :].bitcast(F32), in_=table_sb[:].bitcast(F32))

        def table_to_channels(doubled, table_t, half, tag):
            words = doubled[:].rearrange("p j h d -> p j (h d)").bitcast(F32)
            table_words = table_t[:].rearrange("q s e -> q (s e)").bitcast(F32)
            table_ps = psum_rope.tile([P, GROUP_ROWS, P], F32, tag=tag)
            for j in range(GROUP_ROWS):
                nc.tensor.transpose(table_ps[:, j, :], words[:, half * GROUP_ROWS + j, :], ident_f32[:])
            nc.scalar.copy(out=table_words[:, half * GROUP_TOKENS : (half + 1) * GROUP_TOKENS], in_=table_ps[:].rearrange("q j p -> q (j p)"))

        cos_doubled = const.tile([P, ROWS, H, D], BF16)
        sin_doubled = const.tile([P, ROWS, H, D], BF16)
        cos_t = const.tile([P, S, 2], BF16)
        sin_t = const.tile([P, S, 2], BF16)

        keep_clock(4, psum_proj, "proj11")
        turn_half(0, 0)
        turn_half(0, 1)
        keep_clock(2, psum_proj, "proj11")
        double_table(cos_sb, cos_doubled)
        double_table(sin_sb, sin_doubled)
        turn_weights()
        nc.vector.quantize_mx(out=w_codes[:].bitcast(FP8X4), scales=w_scales[:], in_=w_grouped[:])
        table_to_channels(cos_doubled, cos_t, 0, "rope0")
        table_to_channels(sin_doubled, sin_t, 0, "rope1")
        quantise(0)

        bias_ps = psum_proj.tile([P, P], F32, tag="proj11")
        nc.tensor.transpose(bias_ps[:], bias_row[:].bitcast(F32), ident_f32[:])
        project(0)
        bias_pair = const.tile([P, 2], BF16)
        nc.vector.tensor_copy(out=bias_pair[:].bitcast(F32), in_=bias_ps[:, 0:1])
        bias = const.tile([P, 2], F32)
        nc.vector.tensor_copy(out=bias[:], in_=bias_pair[:])
        turn_group(1)
        keep_clock(2, psum_rope, "rope1")
        table_to_channels(cos_doubled, cos_t, 1, "rope0")
        table_to_channels(sin_doubled, sin_t, 1, "rope1")

        whole = slice(0, GROUP_TOKENS)
        rope_products(0, 0, whole)
        subtract_products(0, whole)
        turn_group(2)
        quantise(1)
        project(1)
        rope_products(0, 1, whole)
        turn_group(3)
        quantise(2)

        for g in range(1, GROUPS + 1):
            ahead = g + AHEAD - 1
            if g + 1 < GROUPS:
                project(g + 1)
            if g < GROUPS - 1:
                rope_products(g, 0, whole)
                subtract_products(g, whole)
            elif g == GROUPS - 1:
                for half in range(2):
                    cols = slice(half * 2 * P, (half + 1) * 2 * P)
                    rope_products(g, 0, cols)
                    subtract_products(g, cols)
                    rope_products(g, 1, cols)
            if g + 2 < GROUPS:
                quantise(g + 2)
            turn_back(g - 1, 0)
            turn_back(g - 1, 1)
            emit(g - 1, 0)
            if ahead < GROUPS:
                turn_half(ahead, 0)
            if g < GROUPS - 1:
                rope_products(g, 1, whole)
            turn_back(g - 1, 2, by_product=[(0, 0), (1, 0)])
            if ahead < GROUPS:
                turn_half(ahead, 1)
            turn_back(g - 1, 3)
            emit(g - 1, 1)
